import numpy as np
import ml_dtypes


def mxq(x, axis, fmt="e4m3"):
    dtype, down = {"e4m3": (ml_dtypes.float8_e4m3fn, 7), "e5m2": (ml_dtypes.float8_e5m2, 14)}[fmt]
    v = np.moveaxis(np.asarray(x, np.float32).astype(ml_dtypes.bfloat16).astype(np.float64), axis, -1)
    blocks = v.reshape(v.shape[:-1] + (-1, 32))
    amax = np.abs(blocks).max(-1, keepdims=True)
    byte = np.maximum(np.where(amax > 0, np.frexp(amax)[1] - 1 + 127, 0) - down, 1)
    scale = np.exp2(byte - 127.0)
    codes = (blocks / scale).astype(np.float32).astype(dtype).astype(np.float64)
    return np.moveaxis((codes * scale).reshape(v.shape), -1, axis)


WIDE = False


def mx_kscale(k):
    if not WIDE:
        return np.ones(k)
    levels = np.array([10, -10, 5, -5, 0])
    a = np.random.permutation(np.resize(levels, k // 512 * 4)).reshape(k // 512, 4)
    idx = np.arange(k)
    return np.exp2(a[idx // 512, idx % 128 // 32])


BF16 = ml_dtypes.bfloat16


def bf(x):
    return np.asarray(x, np.float32).astype(BF16)


def f64(x):
    return np.asarray(x).astype(np.float64)


M, P, D = 16384, 512, 128


def setup_inputs():
    s = mx_kscale(P)
    return {"G": bf(np.exp(-np.abs(3.0 + np.random.standard_normal((M, P)))) * s[None, :]),
            "x_next": bf(np.random.standard_normal((P, D)) * 1.5 * (s.mean() / s)[:, None])}


def reference(G, x_next):
    g = f64(G)
    p = g / np.sum(g, axis=1, keepdims=True)
    return mxq(p, 1, "e4m3") @ mxq(f64(x_next), 0, "e4m3")

@@ -1,0 +1,112 @@
+from contextlib import ExitStack
+
+import concourse.mybir as mybir
+from concourse.masks import make_identity
+
+F32 = mybir.dt.float32
+BF16 = mybir.dt.bfloat16
+U32 = mybir.dt.uint32
+U8 = mybir.dt.uint8
+FP8X4 = mybir.dt.float8_e4m3fn_x4
+MULT = mybir.AluOpType.mult
+ADD = mybir.AluOpType.add
+
+P = 128
+M, K, D = 16384, 512, 128
+PACK = 4
+TILES = M // P
+GROUP = 4
+FLOPS = 2 * M * K * D
+
+
+def tile_nntransformlearner_pb_t_kernel(tc, G, x_next, out):
+    nc = tc.nc
+    g_view = G.rearrange("(p c) k -> p c k", c=TILES)
+    out_view = out.rearrange("(p c) d -> p c d", c=TILES)
+    with ExitStack() as ctx:
+        const = ctx.enter_context(tc.tile_pool(name="const", bufs=1))
+        gpool = ctx.enter_context(tc.tile_pool(name="gpool", bufs=10))
+        small = ctx.enter_context(tc.tile_pool(name="small", bufs=6))
+        ppool = ctx.enter_context(tc.tile_pool(name="ppool", bufs=3))
+        qpool = ctx.enter_context(tc.tile_pool(name="qpool", bufs=3))
+        opool = ctx.enter_context(tc.tile_pool(name="opool", bufs=4))
+        psum_t = ctx.enter_context(tc.psum_pool(name="psum_t", bufs=4))
+        psum_o = ctx.enter_context(tc.psum_pool(name="psum_o", bufs=3))
+
+        ident = const.tile([P, P], BF16)
+        make_identity(nc, ident[:])
+
+        x_raw = const.tile([P, PACK, D], BF16)
+        nc.scalar.dma_start(out=x_raw[:], in_=x_next.rearrange("(t p) d -> p t d", p=P))
+        x_grouped = const.tile([P, D, PACK], BF16, align_bytes=64)
+        nc.vector.tensor_copy(out=x_grouped[:], in_=x_raw[:].rearrange("p t d -> p d t"))
+        x_codes = const.tile([P, D], U32, align_bytes=64)
+        x_scales = const.tile([P, D], U8, align_bytes=64)
+        nc.vector.quantize_mx(
+            out=x_codes[:].bitcast(FP8X4),
+            scales=x_scales[:],
+            in_=x_grouped[:].rearrange("p d t -> p (d t)"),
+        )
+        junk = const.tile([P, K // 2], F32)
+
+        for g in range(TILES // GROUP):
+            cols = slice(g * GROUP, (g + 1) * GROUP)
+            g_sb = gpool.tile([P, GROUP, K], BF16)
+            nc.sync.dma_start(out=g_sb[:], in_=g_view[:, cols, :])
+            sums = small.tile([P, GROUP], F32)
+            for j in range(GROUP):
+                nc.vector.scalar_tensor_tensor(
+                    out=junk[:],
+                    in0=g_sb[:, j, 0 : K // 2],
+                    scalar=1.0,
+                    in1=g_sb[:, j, K // 2 : K],
+                    op0=MULT,
+                    op1=ADD,
+                    accum_out=sums[:, j : j + 1],
+                )
+            recip = small.tile([P, GROUP], F32)
+            nc.vector.reciprocal(recip[:], sums[:])
+            p_sb = ppool.tile([P, GROUP, K], BF16)
+            for j in range(GROUP):
+                nc.vector.tensor_scalar(
+                    out=p_sb[:, j, :],
+                    in0=g_sb[:, j, :],
+                    scalar1=recip[:, j : j + 1],
+                    scalar2=None,
+                    op0=MULT,
+                )
+            grouped = qpool.tile([P, GROUP, P, PACK], BF16, align_bytes=64)
+            for h in range(GROUP // 2):
+                xt = psum_t.tile([P, 2, PACK, P], BF16)
+                for jj in range(2):
+                    for t in range(PACK):
+                        nc.tensor.transpose(
+                            xt[:, jj, t, :],
+                            p_sb[:, 2 * h + jj, t * P : (t + 1) * P],
+                            ident[:],
+                        )
+                nc.scalar.copy(
+                    out=grouped[:, 2 * h : 2 * h + 2, :, :],
+                    in_=xt[:].rearrange("p j t m -> p j m t"),
+                )
+            codes = qpool.tile([P, GROUP * P], U32, align_bytes=64)
+            scales = qpool.tile([P, GROUP * P], U8, align_bytes=64)
+            nc.vector.quantize_mx(
+                out=codes[:].bitcast(FP8X4),
+                scales=scales[:],
+                in_=grouped[:].rearrange("p j m t -> p (j m t)"),
+            )
+            acc = psum_o.tile([P, GROUP, D], F32)
+            for j in range(GROUP):
+                nc.tensor.matmul_mx(
+                    out=acc[:, j, :],
+                    lhsT=codes[:, j * P : (j + 1) * P].bitcast(FP8X4),
+                    lhsT_scale=scales[:, j * P : (j + 1) * P],
+                    rhs=x_codes[:].bitcast(FP8X4),
+                    rhs_scale=x_scales[:],
+                    start=True,
+                    stop=True,
+                )
+            o_sb = opool.tile([P, GROUP, D], F32)
+            nc.scalar.copy(out=o_sb[:], in_=acc[:])
+            nc.sync.dma_start(out=out_view[:, cols, :], in_=o_sb[:])

@@ -16,7 +16,15 @@ M, K, D = 16384, 512, 128
 PACK = 4
 TILES = M // P
 GROUP = 4
+QUADS = TILES // GROUP
 FLOPS = 2 * M * K * D
+
+LAG_T = 2
+LAG_D = 4
+LAG_M = 4
+AHEAD = 8
+DUMMIES = 0
+E_ON_V_EVERY = 0
 
 
 def tile_nntransformlearner_pb_t_kernel(tc, G, x_next, out):
@@ -25,19 +33,117 @@ def tile_nntransformlearner_pb_t_kernel(tc, G, x_next, out):
     out_view = out.rearrange("(p c) d -> p c d", c=TILES)
     with ExitStack() as ctx:
         const = ctx.enter_context(tc.tile_pool(name="const", bufs=1))
-        gpool = ctx.enter_context(tc.tile_pool(name="gpool", bufs=10))
-        small = ctx.enter_context(tc.tile_pool(name="small", bufs=6))
+        gpool = ctx.enter_context(tc.tile_pool(name="gpool", bufs=AHEAD + 2))
+        small = ctx.enter_context(tc.tile_pool(name="small", bufs=4))
         ppool = ctx.enter_context(tc.tile_pool(name="ppool", bufs=3))
-        qpool = ctx.enter_context(tc.tile_pool(name="qpool", bufs=3))
+        qpool = ctx.enter_context(tc.tile_pool(name="qpool", bufs=4))
+        cpool = ctx.enter_context(tc.tile_pool(name="cpool", bufs=3))
         opool = ctx.enter_context(tc.tile_pool(name="opool", bufs=4))
-        psum_t = ctx.enter_context(tc.psum_pool(name="psum_t", bufs=4))
+        psum_t = ctx.enter_context(tc.psum_pool(name="psum_t", bufs=5))
         psum_o = ctx.enter_context(tc.psum_pool(name="psum_o", bufs=3))
+        ctx.enter_context(tc.manual_schedule())
 
-        ident = const.tile([P, P], BF16)
-        make_identity(nc, ident[:])
+        g_tiles = {}
+        sums_t = {}
+        recip_t = {}
+        p_tiles = {}
+        grouped_t = {}
+        codes_t = {}
+        scales_t = {}
+        acc_t = {}
+
+        def load(q):
+            g_sb = gpool.tile([P, GROUP, K], BF16, name="g_sb")
+            g_tiles[q] = g_sb
+            if q == 0:
+                for j in range(GROUP):
+                    nc.sync.dma_start(out=g_sb[:, j, :], in_=g_view[:, j, :])
+            else:
+                nc.sync.dma_start(out=g_sb[:], in_=g_view[:, q * GROUP : (q + 1) * GROUP, :])
+
+        def row_sums(q):
+            sums = small.tile([P, GROUP], F32, name="sums")
+            sums_t[q] = sums
+            for j in range(GROUP):
+                nc.vector.scalar_tensor_tensor(
+                    out=junk[:, j, :],
+                    in0=g_tiles[q][:, j, 0 : K // 2],
+                    scalar=1.0,
+                    in1=g_tiles[q][:, j, K // 2 : K],
+                    op0=MULT,
+                    op1=ADD,
+                    accum_out=sums[:, j : j + 1],
+                )
+
+        def reciprocals(q):
+            recip = small.tile([P, GROUP], F32, name="recip")
+            recip_t[q] = recip
+            nc.vector.reciprocal(recip[:], sums_t[q][:])
+
+        def normalise(q):
+            p_sb = ppool.tile([P, GROUP, K], BF16, name="p_sb")
+            p_tiles[q] = p_sb
+            for j in range(GROUP):
+                nc.vector.tensor_scalar(
+                    out=p_sb[:, j, :],
+                    in0=g_tiles[q][:, j, :],
+                    scalar1=recip_t[q][:, j : j + 1],
+                    scalar2=None,
+                    op0=MULT,
+                )
+
+        def transpose_and_regroup(q):
+            grouped = qpool.tile([P, GROUP, P, PACK], BF16, name="grouped", align_bytes=64)
+            grouped_t[q] = grouped
+            xts = []
+            for j in range(GROUP):
+                xt = psum_t.tile([P, PACK, P], BF16, name="xt")
+                xts.append(xt)
+                for t in range(PACK):
+                    nc.tensor.transpose(xt[:, t, :], p_tiles[q][:, j, t * P : (t + 1) * P], ident[:])
+            for j in range(GROUP):
+                nc.scalar.copy(out=grouped[:, j, :, :], in_=xts[j][:].rearrange("p t m -> p m t"))
+
+        def quantise(q):
+            codes = cpool.tile([P, GROUP * P], U32, name="codes", align_bytes=64)
+            scales = cpool.tile([P, GROUP * P], U8, name="scales", align_bytes=64)
+            codes_t[q] = codes
+            scales_t[q] = scales
+            nc.vector.quantize_mx(
+                out=codes[:].bitcast(FP8X4),
+                scales=scales[:],
+                in_=grouped_t[q][:].rearrange("p j m t -> p (j m t)"),
+            )
+
+        def multiply(q):
+            acc = psum_o.tile([P, GROUP, D], F32, name="acc")
+            acc_t[q] = acc
+            for j in range(GROUP):
+                nc.tensor.matmul_mx(
+                    out=acc[:, j, :],
+                    lhsT=codes_t[q][:, j * P : (j + 1) * P].bitcast(FP8X4),
+                    lhsT_scale=scales_t[q][:, j * P : (j + 1) * P],
+                    rhs=x_codes[:].bitcast(FP8X4),
+                    rhs_scale=x_scales[:],
+                    start=True,
+                    stop=True,
+                )
+
+        def store(q):
+            o_sb = opool.tile([P, GROUP, D], F32, name="o_sb")
+            if E_ON_V_EVERY and q % E_ON_V_EVERY == E_ON_V_EVERY - 1:
+                nc.vector.tensor_copy(out=o_sb[:], in_=acc_t[q][:])
+            else:
+                nc.scalar.copy(out=o_sb[:], in_=acc_t[q][:])
+            nc.sync.dma_start(out=out_view[:, q * GROUP : (q + 1) * GROUP, :], in_=o_sb[:])
 
         x_raw = const.tile([P, PACK, D], BF16)
         nc.scalar.dma_start(out=x_raw[:], in_=x_next.rearrange("(t p) d -> p t d", p=P))
+        for q in range(AHEAD):
+            load(q)
+        ident = const.tile([P, P], BF16)
+        make_identity(nc, ident[:])
+        junk = const.tile([P, GROUP, K // 2], F32)
         x_grouped = const.tile([P, D, PACK], BF16, align_bytes=64)
         nc.vector.tensor_copy(out=x_grouped[:], in_=x_raw[:].rearrange("p t d -> p d t"))
         x_codes = const.tile([P, D], U32, align_bytes=64)
@@ -47,66 +153,20 @@ def tile_nntransformlearner_pb_t_kernel(tc, G, x_next, out):
             scales=x_scales[:],
             in_=x_grouped[:].rearrange("p d t -> p (d t)"),
         )
-        junk = const.tile([P, K // 2], F32)
 
-        for g in range(TILES // GROUP):
-            cols = slice(g * GROUP, (g + 1) * GROUP)
-            g_sb = gpool.tile([P, GROUP, K], BF16)
-            nc.sync.dma_start(out=g_sb[:], in_=g_view[:, cols, :])
-            sums = small.tile([P, GROUP], F32)
-            for j in range(GROUP):
-                nc.vector.scalar_tensor_tensor(
-                    out=junk[:],
-                    in0=g_sb[:, j, 0 : K // 2],
-                    scalar=1.0,
-                    in1=g_sb[:, j, K // 2 : K],
-                    op0=MULT,
-                    op1=ADD,
-                    accum_out=sums[:, j : j + 1],
-                )
-            recip = small.tile([P, GROUP], F32)
-            nc.vector.reciprocal(recip[:], sums[:])
-            p_sb = ppool.tile([P, GROUP, K], BF16)
-            for j in range(GROUP):
-                nc.vector.tensor_scalar(
-                    out=p_sb[:, j, :],
-                    in0=g_sb[:, j, :],
-                    scalar1=recip[:, j : j + 1],
-                    scalar2=None,
-                    op0=MULT,
-                )
-            grouped = qpool.tile([P, GROUP, P, PACK], BF16, align_bytes=64)
-            for h in range(GROUP // 2):
-                xt = psum_t.tile([P, 2, PACK, P], BF16)
-                for jj in range(2):
-                    for t in range(PACK):
-                        nc.tensor.transpose(
-                            xt[:, jj, t, :],
-                            p_sb[:, 2 * h + jj, t * P : (t + 1) * P],
-                            ident[:],
-                        )
-                nc.scalar.copy(
-                    out=grouped[:, 2 * h : 2 * h + 2, :, :],
-                    in_=xt[:].rearrange("p j t m -> p j m t"),
-                )
-            codes = qpool.tile([P, GROUP * P], U32, align_bytes=64)
-            scales = qpool.tile([P, GROUP * P], U8, align_bytes=64)
-            nc.vector.quantize_mx(
-                out=codes[:].bitcast(FP8X4),
-                scales=scales[:],
-                in_=grouped[:].rearrange("p j m t -> p (j m t)"),
-            )
-            acc = psum_o.tile([P, GROUP, D], F32)
-            for j in range(GROUP):
-                nc.tensor.matmul_mx(
-                    out=acc[:, j, :],
-                    lhsT=codes[:, j * P : (j + 1) * P].bitcast(FP8X4),
-                    lhsT_scale=scales[:, j * P : (j + 1) * P],
-                    rhs=x_codes[:].bitcast(FP8X4),
-                    rhs_scale=x_scales[:],
-                    start=True,
-                    stop=True,
-                )
-            o_sb = opool.tile([P, GROUP, D], F32)
-            nc.scalar.copy(out=o_sb[:], in_=acc[:])
-            nc.sync.dma_start(out=out_view[:, cols, :], in_=o_sb[:])
+        for s in range(QUADS + LAG_M):
+            if s + AHEAD < QUADS:
+                load(s + AHEAD)
+            if s < QUADS:
+                row_sums(s)
+            if 0 <= s - LAG_D < QUADS:
+                quantise(s - LAG_D)
+            if s < QUADS:
+                reciprocals(s)
+            if 0 <= s - 1 < QUADS:
+                normalise(s - 1)
+            if 0 <= s - LAG_T < QUADS:
+                transpose_and_regroup(s - LAG_T)
+            if 0 <= s - LAG_M < QUADS:
+                multiply(s - LAG_M)
+                store(s - LAG_M)

@@ -19,12 +19,12 @@ GROUP = 4
 QUADS = TILES // GROUP
 FLOPS = 2 * M * K * D
 
-LAG_T = 2
-LAG_D = 4
-LAG_M = 4
+LAG_D = 2
+LAG_M = 2
 AHEAD = 8
-DUMMIES = 0
-E_ON_V_EVERY = 0
+E_ON_V_EVERY = 4
+C_ON_V_EVERY = 0
+TAIL_V = 2
 
 
 def tile_nntransformlearner_pb_t_kernel(tc, G, x_next, out):
@@ -47,10 +47,21 @@ def tile_nntransformlearner_pb_t_kernel(tc, G, x_next, out):
         sums_t = {}
         recip_t = {}
         p_tiles = {}
+        xt_t = {}
         grouped_t = {}
         codes_t = {}
         scales_t = {}
         acc_t = {}
+
+        def e_on_vector(q):
+            if q >= QUADS - TAIL_V:
+                return True
+            return E_ON_V_EVERY > 0 and q % E_ON_V_EVERY == E_ON_V_EVERY - 1
+
+        def c_on_vector(n):
+            if n >= TILES - GROUP * TAIL_V:
+                return n % 2 == 1
+            return C_ON_V_EVERY > 0 and n % C_ON_V_EVERY == C_ON_V_EVERY - 1
 
         def load(q):
             g_sb = gpool.tile([P, GROUP, K], BF16, name="g_sb")
@@ -61,66 +72,60 @@ def tile_nntransformlearner_pb_t_kernel(tc, G, x_next, out):
             else:
                 nc.sync.dma_start(out=g_sb[:], in_=g_view[:, q * GROUP : (q + 1) * GROUP, :])
 
-        def row_sums(q):
-            sums = small.tile([P, GROUP], F32, name="sums")
-            sums_t[q] = sums
-            for j in range(GROUP):
-                nc.vector.scalar_tensor_tensor(
-                    out=junk[:, j, :],
-                    in0=g_tiles[q][:, j, 0 : K // 2],
-                    scalar=1.0,
-                    in1=g_tiles[q][:, j, K // 2 : K],
-                    op0=MULT,
-                    op1=ADD,
-                    accum_out=sums[:, j : j + 1],
-                )
+        def row_sum(n):
+            q, j = divmod(n, GROUP)
+            if j == 0:
+                sums_t[q] = small.tile([P, GROUP], F32, name="sums")
+            nc.vector.scalar_tensor_tensor(
+                out=junk[:, j, :],
+                in0=g_tiles[q][:, j, 0 : K // 2],
+                scalar=1.0,
+                in1=g_tiles[q][:, j, K // 2 : K],
+                op0=MULT,
+                op1=ADD,
+                accum_out=sums_t[q][:, j : j + 1],
+            )
 
         def reciprocals(q):
-            recip = small.tile([P, GROUP], F32, name="recip")
-            recip_t[q] = recip
-            nc.vector.reciprocal(recip[:], sums_t[q][:])
+            recip_t[q] = small.tile([P, GROUP], F32, name="recip")
+            nc.vector.reciprocal(recip_t[q][:], sums_t[q][:])
 
         def normalise(q):
-            p_sb = ppool.tile([P, GROUP, K], BF16, name="p_sb")
-            p_tiles[q] = p_sb
+            p_tiles[q] = ppool.tile([P, GROUP, K], BF16, name="p_sb")
             for j in range(GROUP):
                 nc.vector.tensor_scalar(
-                    out=p_sb[:, j, :],
+                    out=p_tiles[q][:, j, :],
                     in0=g_tiles[q][:, j, :],
                     scalar1=recip_t[q][:, j : j + 1],
                     scalar2=None,
                     op0=MULT,
                 )
 
-        def transpose_and_regroup(q):
-            grouped = qpool.tile([P, GROUP, P, PACK], BF16, name="grouped", align_bytes=64)
-            grouped_t[q] = grouped
-            xts = []
+        def transpose(q):
             for j in range(GROUP):
                 xt = psum_t.tile([P, PACK, P], BF16, name="xt")
-                xts.append(xt)
+                xt_t[q * GROUP + j] = xt
                 for t in range(PACK):
                     nc.tensor.transpose(xt[:, t, :], p_tiles[q][:, j, t * P : (t + 1) * P], ident[:])
-            for j in range(GROUP):
-                nc.scalar.copy(out=grouped[:, j, :, :], in_=xts[j][:].rearrange("p t m -> p m t"))
+
+        def regroup(n, engine_copy):
+            q, j = divmod(n, GROUP)
+            engine_copy(out=grouped_t[q][:, j, :, :], in_=xt_t[n][:].rearrange("p t m -> p m t"))
 
         def quantise(q):
-            codes = cpool.tile([P, GROUP * P], U32, name="codes", align_bytes=64)
-            scales = cpool.tile([P, GROUP * P], U8, name="scales", align_bytes=64)
-            codes_t[q] = codes
-            scales_t[q] = scales
+            codes_t[q] = cpool.tile([P, GROUP * P], U32, name="codes", align_bytes=64)
+            scales_t[q] = cpool.tile([P, GROUP * P], U8, name="scales", align_bytes=64)
             nc.vector.quantize_mx(
-                out=codes[:].bitcast(FP8X4),
-                scales=scales[:],
+                out=codes_t[q][:].bitcast(FP8X4),
+                scales=scales_t[q][:],
                 in_=grouped_t[q][:].rearrange("p j m t -> p (j m t)"),
             )
 
         def multiply(q):
-            acc = psum_o.tile([P, GROUP, D], F32, name="acc")
-            acc_t[q] = acc
+            acc_t[q] = psum_o.tile([P, GROUP, D], F32, name="acc")
             for j in range(GROUP):
                 nc.tensor.matmul_mx(
-                    out=acc[:, j, :],
+                    out=acc_t[q][:, j, :],
                     lhsT=codes_t[q][:, j * P : (j + 1) * P].bitcast(FP8X4),
                     lhsT_scale=scales_t[q][:, j * P : (j + 1) * P],
                     rhs=x_codes[:].bitcast(FP8X4),
@@ -129,12 +134,9 @@ def tile_nntransformlearner_pb_t_kernel(tc, G, x_next, out):
                     stop=True,
                 )
 
-        def store(q):
+        def store(q, engine_copy):
             o_sb = opool.tile([P, GROUP, D], F32, name="o_sb")
-            if E_ON_V_EVERY and q % E_ON_V_EVERY == E_ON_V_EVERY - 1:
-                nc.vector.tensor_copy(out=o_sb[:], in_=acc_t[q][:])
-            else:
-                nc.scalar.copy(out=o_sb[:], in_=acc_t[q][:])
+            engine_copy(out=o_sb[:], in_=acc_t[q][:])
             nc.sync.dma_start(out=out_view[:, q * GROUP : (q + 1) * GROUP, :], in_=o_sb[:])
 
         x_raw = const.tile([P, PACK, D], BF16)
@@ -145,28 +147,45 @@ def tile_nntransformlearner_pb_t_kernel(tc, G, x_next, out):
         make_identity(nc, ident[:])
         junk = const.tile([P, GROUP, K // 2], F32)
         x_grouped = const.tile([P, D, PACK], BF16, align_bytes=64)
-        nc.vector.tensor_copy(out=x_grouped[:], in_=x_raw[:].rearrange("p t d -> p d t"))
         x_codes = const.tile([P, D], U32, align_bytes=64)
         x_scales = const.tile([P, D], U8, align_bytes=64)
-        nc.vector.quantize_mx(
-            out=x_codes[:].bitcast(FP8X4),
-            scales=x_scales[:],
-            in_=x_grouped[:].rearrange("p d t -> p (d t)"),
-        )
 
-        for s in range(QUADS + LAG_M):
+        row_sum(0)
+        for s in range(QUADS + LAG_M + 2):
             if s + AHEAD < QUADS:
                 load(s + AHEAD)
             if s < QUADS:
-                row_sums(s)
+                for j in range(1, GROUP):
+                    row_sum(s * GROUP + j)
+            if 0 <= s - 1 < QUADS:
+                for j in range(GROUP):
+                    if c_on_vector((s - 1) * GROUP + j):
+                        regroup((s - 1) * GROUP + j, nc.vector.tensor_copy)
+            if 0 <= s - LAG_M - 1 < QUADS and e_on_vector(s - LAG_M - 1):
+                store(s - LAG_M - 1, nc.vector.tensor_copy)
             if 0 <= s - LAG_D < QUADS:
                 quantise(s - LAG_D)
             if s < QUADS:
                 reciprocals(s)
-            if 0 <= s - 1 < QUADS:
-                normalise(s - 1)
-            if 0 <= s - LAG_T < QUADS:
-                transpose_and_regroup(s - LAG_T)
+            if s + 1 < QUADS:
+                row_sum((s + 1) * GROUP)
+            if s < QUADS:
+                normalise(s)
+            if s == 0:
+                nc.vector.tensor_copy(out=x_grouped[:], in_=x_raw[:].rearrange("p t d -> p d t"))
+            if s == 1:
+                nc.vector.quantize_mx(
+                    out=x_codes[:].bitcast(FP8X4),
+                    scales=x_scales[:],
+                    in_=x_grouped[:].rearrange("p d t -> p (d t)"),
+                )
             if 0 <= s - LAG_M < QUADS:
                 multiply(s - LAG_M)
-                store(s - LAG_M)
+                if not e_on_vector(s - LAG_M):
+                    store(s - LAG_M, nc.scalar.copy)
+            if s < QUADS:
+                transpose(s)
+                grouped_t[s] = qpool.tile([P, GROUP, P, PACK], BF16, name="grouped", align_bytes=64)
+                for j in range(GROUP):
+                    if not c_on_vector(s * GROUP + j):
+                        regroup(s * GROUP + j, nc.scalar.copy)

@@ -22,7 +22,7 @@ FLOPS = 2 * M * K * D
 LAG_D = 2
 LAG_M = 2
 AHEAD = 8
-E_ON_V_EVERY = 4
+E_ON_V_EVERY = 0
 C_ON_V_EVERY = 0
 TAIL_V = 2
 

@@ -19,12 +19,11 @@ GROUP = 4
 QUADS = TILES // GROUP
 FLOPS = 2 * M * K * D
 
-LAG_D = 2
-LAG_M = 2
+LAG = 4
 AHEAD = 8
+TAIL_C = 1
+TAIL_E = 3
 E_ON_V_EVERY = 0
-C_ON_V_EVERY = 0
-TAIL_V = 2
 
 
 def tile_nntransformlearner_pb_t_kernel(tc, G, x_next, out):
@@ -36,7 +35,7 @@ def tile_nntransformlearner_pb_t_kernel(tc, G, x_next, out):
         gpool = ctx.enter_context(tc.tile_pool(name="gpool", bufs=AHEAD + 2))
         small = ctx.enter_context(tc.tile_pool(name="small", bufs=4))
         ppool = ctx.enter_context(tc.tile_pool(name="ppool", bufs=3))
-        qpool = ctx.enter_context(tc.tile_pool(name="qpool", bufs=4))
+        qpool = ctx.enter_context(tc.tile_pool(name="qpool", bufs=LAG + 2))
         cpool = ctx.enter_context(tc.tile_pool(name="cpool", bufs=3))
         opool = ctx.enter_context(tc.tile_pool(name="opool", bufs=4))
         psum_t = ctx.enter_context(tc.psum_pool(name="psum_t", bufs=5))
@@ -54,14 +53,12 @@ def tile_nntransformlearner_pb_t_kernel(tc, G, x_next, out):
         acc_t = {}
 
         def e_on_vector(q):
-            if q >= QUADS - TAIL_V:
+            if q >= QUADS - TAIL_E:
                 return True
             return E_ON_V_EVERY > 0 and q % E_ON_V_EVERY == E_ON_V_EVERY - 1
 
         def c_on_vector(n):
-            if n >= TILES - GROUP * TAIL_V:
-                return n % 2 == 1
-            return C_ON_V_EVERY > 0 and n % C_ON_V_EVERY == C_ON_V_EVERY - 1
+            return n >= TILES - GROUP * TAIL_C and n % 2 == 1
 
         def load(q):
             g_sb = gpool.tile([P, GROUP, K], BF16, name="g_sb")
@@ -76,6 +73,8 @@ def tile_nntransformlearner_pb_t_kernel(tc, G, x_next, out):
             q, j = divmod(n, GROUP)
             if j == 0:
                 sums_t[q] = small.tile([P, GROUP], F32, name="sums")
+                recip_t[q] = small.tile([P, GROUP], F32, name="recip")
+                p_tiles[q] = ppool.tile([P, GROUP, K], BF16, name="p_sb")
             nc.vector.scalar_tensor_tensor(
                 out=junk[:, j, :],
                 in0=g_tiles[q][:, j, 0 : K // 2],
@@ -86,27 +85,25 @@ def tile_nntransformlearner_pb_t_kernel(tc, G, x_next, out):
                 accum_out=sums_t[q][:, j : j + 1],
             )
 
-        def reciprocals(q):
-            recip_t[q] = small.tile([P, GROUP], F32, name="recip")
-            nc.vector.reciprocal(recip_t[q][:], sums_t[q][:])
+        def reciprocals(q, first, last):
+            nc.vector.reciprocal(recip_t[q][:, first:last], sums_t[q][:, first:last])
 
-        def normalise(q):
-            p_tiles[q] = ppool.tile([P, GROUP, K], BF16, name="p_sb")
-            for j in range(GROUP):
-                nc.vector.tensor_scalar(
-                    out=p_tiles[q][:, j, :],
-                    in0=g_tiles[q][:, j, :],
-                    scalar1=recip_t[q][:, j : j + 1],
-                    scalar2=None,
-                    op0=MULT,
-                )
+        def normalise(n):
+            q, j = divmod(n, GROUP)
+            nc.vector.tensor_scalar(
+                out=p_tiles[q][:, j, :],
+                in0=g_tiles[q][:, j, :],
+                scalar1=recip_t[q][:, j : j + 1],
+                scalar2=None,
+                op0=MULT,
+            )
 
-        def transpose(q):
-            for j in range(GROUP):
-                xt = psum_t.tile([P, PACK, P], BF16, name="xt")
-                xt_t[q * GROUP + j] = xt
-                for t in range(PACK):
-                    nc.tensor.transpose(xt[:, t, :], p_tiles[q][:, j, t * P : (t + 1) * P], ident[:])
+        def transpose(n):
+            q, j = divmod(n, GROUP)
+            xt = psum_t.tile([P, PACK, P], BF16, name="xt")
+            xt_t[n] = xt
+            for t in range(PACK):
+                nc.tensor.transpose(xt[:, t, :], p_tiles[q][:, j, t * P : (t + 1) * P], ident[:])
 
         def regroup(n, engine_copy):
             q, j = divmod(n, GROUP)
@@ -151,26 +148,31 @@ def tile_nntransformlearner_pb_t_kernel(tc, G, x_next, out):
         x_scales = const.tile([P, D], U8, align_bytes=64)
 
         row_sum(0)
-        for s in range(QUADS + LAG_M + 2):
+        for s in range(QUADS + LAG + 2):
             if s + AHEAD < QUADS:
                 load(s + AHEAD)
-            if s < QUADS:
+            if s == 0:
+                for j in range(GROUP):
+                    row_sum(j + 1)
+                    reciprocals(0, j, j + 1)
+                    normalise(j)
+            elif s < QUADS:
                 for j in range(1, GROUP):
                     row_sum(s * GROUP + j)
+            if 0 <= s - LAG < QUADS:
+                quantise(s - LAG)
             if 0 <= s - 1 < QUADS:
                 for j in range(GROUP):
                     if c_on_vector((s - 1) * GROUP + j):
                         regroup((s - 1) * GROUP + j, nc.vector.tensor_copy)
-            if 0 <= s - LAG_M - 1 < QUADS and e_on_vector(s - LAG_M - 1):
-                store(s - LAG_M - 1, nc.vector.tensor_copy)
-            if 0 <= s - LAG_D < QUADS:
-                quantise(s - LAG_D)
-            if s < QUADS:
-                reciprocals(s)
-            if s + 1 < QUADS:
-                row_sum((s + 1) * GROUP)
-            if s < QUADS:
-                normalise(s)
+            if 0 <= s - LAG - 1 < QUADS and e_on_vector(s - LAG - 1):
+                store(s - LAG - 1, nc.vector.tensor_copy)
+            if 0 < s < QUADS:
+                reciprocals(s, 0, GROUP)
+                if s + 1 < QUADS:
+                    row_sum((s + 1) * GROUP)
+                for j in range(GROUP):
+                    normalise(s * GROUP + j)
             if s == 0:
                 nc.vector.tensor_copy(out=x_grouped[:], in_=x_raw[:].rearrange("p t d -> p d t"))
             if s == 1:
@@ -179,13 +181,14 @@ def tile_nntransformlearner_pb_t_kernel(tc, G, x_next, out):
                     scales=x_scales[:],
                     in_=x_grouped[:].rearrange("p d t -> p (d t)"),
                 )
-            if 0 <= s - LAG_M < QUADS:
-                multiply(s - LAG_M)
-                if not e_on_vector(s - LAG_M):
-                    store(s - LAG_M, nc.scalar.copy)
+            if 0 <= s - LAG < QUADS:
+                multiply(s - LAG)
+                if not e_on_vector(s - LAG):
+                    store(s - LAG, nc.scalar.copy)
             if s < QUADS:
-                transpose(s)
                 grouped_t[s] = qpool.tile([P, GROUP, P, PACK], BF16, name="grouped", align_bytes=64)
+                for j in range(GROUP):
+                    transpose(s * GROUP + j)
                 for j in range(GROUP):
                     if not c_on_vector(s * GROUP + j):
                         regroup(s * GROUP + j, nc.scalar.copy)

@@ -22,8 +22,12 @@ FLOPS = 2 * M * K * D
 LAG = 4
 AHEAD = 8
 TAIL_C = 1
-TAIL_E = 3
+TAIL_E = 1
 E_ON_V_EVERY = 0
+S_SUM_TILE = 1
+S_SUM_EVERY = 5
+S_SUM_AHEAD = 2
+COPY = mybir.ActivationFunctionType.Copy
 
 
 def tile_nntransformlearner_pb_t_kernel(tc, G, x_next, out):
@@ -33,7 +37,7 @@ def tile_nntransformlearner_pb_t_kernel(tc, G, x_next, out):
     with ExitStack() as ctx:
         const = ctx.enter_context(tc.tile_pool(name="const", bufs=1))
         gpool = ctx.enter_context(tc.tile_pool(name="gpool", bufs=AHEAD + 2))
-        small = ctx.enter_context(tc.tile_pool(name="small", bufs=4))
+        small = ctx.enter_context(tc.tile_pool(name="small", bufs=6))
         ppool = ctx.enter_context(tc.tile_pool(name="ppool", bufs=3))
         qpool = ctx.enter_context(tc.tile_pool(name="qpool", bufs=LAG + 2))
         cpool = ctx.enter_context(tc.tile_pool(name="cpool", bufs=3))
@@ -60,6 +64,12 @@ def tile_nntransformlearner_pb_t_kernel(tc, G, x_next, out):
         def c_on_vector(n):
             return n >= TILES - GROUP * TAIL_C and n % 2 == 1
 
+        def sum_on_scalar(n):
+            q, j = divmod(n, GROUP)
+            if j != S_SUM_TILE or q == 0 or q >= QUADS:
+                return False
+            return q <= 2 or q % S_SUM_EVERY == S_SUM_EVERY - 1
+
         def load(q):
             g_sb = gpool.tile([P, GROUP, K], BF16, name="g_sb")
             g_tiles[q] = g_sb
@@ -69,12 +79,25 @@ def tile_nntransformlearner_pb_t_kernel(tc, G, x_next, out):
             else:
                 nc.sync.dma_start(out=g_sb[:], in_=g_view[:, q * GROUP : (q + 1) * GROUP, :])
 
+        def new_quad(q):
+            sums_t[q] = small.tile([P, GROUP, 8], F32, name="sums")
+            recip_t[q] = small.tile([P, GROUP], F32, name="recip")
+
+        def row_sum_scalar(n):
+            q, j = divmod(n, GROUP)
+            nc.scalar.activation(
+                out=junk_s[:, q % 2, :],
+                in_=g_tiles[q][:, j, :],
+                func=COPY,
+                accum_out=sums_t[q][:, j, 0:1],
+            )
+
         def row_sum(n):
             q, j = divmod(n, GROUP)
             if j == 0:
-                sums_t[q] = small.tile([P, GROUP], F32, name="sums")
-                recip_t[q] = small.tile([P, GROUP], F32, name="recip")
                 p_tiles[q] = ppool.tile([P, GROUP, K], BF16, name="p_sb")
+            if sum_on_scalar(n):
+                return
             nc.vector.scalar_tensor_tensor(
                 out=junk[:, j, :],
                 in0=g_tiles[q][:, j, 0 : K // 2],
@@ -82,11 +105,11 @@ def tile_nntransformlearner_pb_t_kernel(tc, G, x_next, out):
                 in1=g_tiles[q][:, j, K // 2 : K],
                 op0=MULT,
                 op1=ADD,
-                accum_out=sums_t[q][:, j : j + 1],
+                accum_out=sums_t[q][:, j, 0:1],
             )
 
         def reciprocals(q, first, last):
-            nc.vector.reciprocal(recip_t[q][:, first:last], sums_t[q][:, first:last])
+            nc.vector.reciprocal(recip_t[q][:, first:last], sums_t[q][:, first:last, 0])
 
         def normalise(n):
             q, j = divmod(n, GROUP)
@@ -143,14 +166,26 @@ def tile_nntransformlearner_pb_t_kernel(tc, G, x_next, out):
         ident = const.tile([P, P], BF16)
         make_identity(nc, ident[:])
         junk = const.tile([P, GROUP, K // 2], F32)
+        junk_s = const.tile([P, 2, K], BF16)
         x_grouped = const.tile([P, D, PACK], BF16, align_bytes=64)
         x_codes = const.tile([P, D], U32, align_bytes=64)
         x_scales = const.tile([P, D], U8, align_bytes=64)
 
+        nc.scalar.copy(out=x_grouped[:], in_=x_raw[:].rearrange("p t d -> p d t"))
+        for q in range(S_SUM_AHEAD):
+            new_quad(q)
+            for j in range(GROUP):
+                if sum_on_scalar(q * GROUP + j):
+                    row_sum_scalar(q * GROUP + j)
         row_sum(0)
         for s in range(QUADS + LAG + 2):
             if s + AHEAD < QUADS:
                 load(s + AHEAD)
+            if s + S_SUM_AHEAD < QUADS:
+                new_quad(s + S_SUM_AHEAD)
+                for j in range(GROUP):
+                    if sum_on_scalar((s + S_SUM_AHEAD) * GROUP + j):
+                        row_sum_scalar((s + S_SUM_AHEAD) * GROUP + j)
             if s == 0:
                 for j in range(GROUP):
                     row_sum(j + 1)
@@ -173,8 +208,6 @@ def tile_nntransformlearner_pb_t_kernel(tc, G, x_next, out):
                     row_sum((s + 1) * GROUP)
                 for j in range(GROUP):
                     normalise(s * GROUP + j)
-            if s == 0:
-                nc.vector.tensor_copy(out=x_grouped[:], in_=x_raw[:].rearrange("p t d -> p d t"))
             if s == 1:
                 nc.vector.quantize_mx(
                     out=x_codes[:].bitcast(FP8X4),

@@ -25,7 +25,7 @@ TAIL_C = 1
 TAIL_E = 1
 E_ON_V_EVERY = 0
 S_SUM_TILE = 1
-S_SUM_EVERY = 5
+S_SUM_EVERY = 8
 S_SUM_AHEAD = 2
 COPY = mybir.ActivationFunctionType.Copy
 
@@ -69,6 +69,11 @@ def tile_nntransformlearner_pb_t_kernel(tc, G, x_next, out):
             if j != S_SUM_TILE or q == 0 or q >= QUADS:
                 return False
             return q <= 2 or q % S_SUM_EVERY == S_SUM_EVERY - 1
+
+        def pieces(q):
+            if q == QUADS - 1:
+                return [(0, GROUP // 2), (GROUP // 2, GROUP)]
+            return [(0, GROUP)]
 
         def load(q):
             g_sb = gpool.tile([P, GROUP, K], BF16, name="g_sb")
@@ -132,20 +137,21 @@ def tile_nntransformlearner_pb_t_kernel(tc, G, x_next, out):
             q, j = divmod(n, GROUP)
             engine_copy(out=grouped_t[q][:, j, :, :], in_=xt_t[n][:].rearrange("p t m -> p m t"))
 
-        def quantise(q):
-            codes_t[q] = cpool.tile([P, GROUP * P], U32, name="codes", align_bytes=64)
-            scales_t[q] = cpool.tile([P, GROUP * P], U8, name="scales", align_bytes=64)
+        def quantise(q, first, last):
+            if first == 0:
+                codes_t[q] = cpool.tile([P, GROUP * P], U32, name="codes", align_bytes=64)
+                scales_t[q] = cpool.tile([P, GROUP * P], U8, name="scales", align_bytes=64)
             nc.vector.quantize_mx(
-                out=codes_t[q][:].bitcast(FP8X4),
-                scales=scales_t[q][:],
-                in_=grouped_t[q][:].rearrange("p j m t -> p (j m t)"),
+                out=codes_t[q][:, first * P : last * P].bitcast(FP8X4),
+                scales=scales_t[q][:, first * P : last * P],
+                in_=grouped_t[q][:, first:last, :, :].rearrange("p j m t -> p (j m t)"),
             )
 
-        def multiply(q):
-            acc_t[q] = psum_o.tile([P, GROUP, D], F32, name="acc")
-            for j in range(GROUP):
+        def multiply(q, first, last):
+            acc_t[q, first] = psum_o.tile([P, GROUP, D], F32, name="acc")
+            for j in range(first, last):
                 nc.tensor.matmul_mx(
-                    out=acc_t[q][:, j, :],
+                    out=acc_t[q, first][:, j, :],
                     lhsT=codes_t[q][:, j * P : (j + 1) * P].bitcast(FP8X4),
                     lhsT_scale=scales_t[q][:, j * P : (j + 1) * P],
                     rhs=x_codes[:].bitcast(FP8X4),
@@ -154,15 +160,18 @@ def tile_nntransformlearner_pb_t_kernel(tc, G, x_next, out):
                     stop=True,
                 )
 
-        def store(q, engine_copy):
+        def store(q, first, last, engine_copy):
             o_sb = opool.tile([P, GROUP, D], F32, name="o_sb")
-            engine_copy(out=o_sb[:], in_=acc_t[q][:])
-            nc.sync.dma_start(out=out_view[:, q * GROUP : (q + 1) * GROUP, :], in_=o_sb[:])
+            engine_copy(out=o_sb[:, first:last, :], in_=acc_t[q, first][:, first:last, :])
+            nc.sync.dma_start(
+                out=out_view[:, q * GROUP + first : q * GROUP + last, :], in_=o_sb[:, first:last, :]
+            )
 
         x_raw = const.tile([P, PACK, D], BF16)
-        nc.scalar.dma_start(out=x_raw[:], in_=x_next.rearrange("(t p) d -> p t d", p=P))
         for q in range(AHEAD):
             load(q)
+            if q == 1:
+                nc.sync.dma_start(out=x_raw[:], in_=x_next.rearrange("(t p) d -> p t d", p=P))
         ident = const.tile([P, P], BF16)
         make_identity(nc, ident[:])
         junk = const.tile([P, GROUP, K // 2], F32)
@@ -171,7 +180,6 @@ def tile_nntransformlearner_pb_t_kernel(tc, G, x_next, out):
         x_codes = const.tile([P, D], U32, align_bytes=64)
         x_scales = const.tile([P, D], U8, align_bytes=64)
 
-        nc.scalar.copy(out=x_grouped[:], in_=x_raw[:].rearrange("p t d -> p d t"))
         for q in range(S_SUM_AHEAD):
             new_quad(q)
             for j in range(GROUP):
@@ -195,29 +203,32 @@ def tile_nntransformlearner_pb_t_kernel(tc, G, x_next, out):
                 for j in range(1, GROUP):
                     row_sum(s * GROUP + j)
             if 0 <= s - LAG < QUADS:
-                quantise(s - LAG)
+                for first, last in pieces(s - LAG):
+                    quantise(s - LAG, first, last)
             if 0 <= s - 1 < QUADS:
                 for j in range(GROUP):
                     if c_on_vector((s - 1) * GROUP + j):
                         regroup((s - 1) * GROUP + j, nc.vector.tensor_copy)
             if 0 <= s - LAG - 1 < QUADS and e_on_vector(s - LAG - 1):
-                store(s - LAG - 1, nc.vector.tensor_copy)
+                first, last = pieces(s - LAG - 1)[-1]
+                store(s - LAG - 1, first, last, nc.vector.tensor_copy)
             if 0 < s < QUADS:
                 reciprocals(s, 0, GROUP)
                 if s + 1 < QUADS:
                     row_sum((s + 1) * GROUP)
                 for j in range(GROUP):
                     normalise(s * GROUP + j)
-            if s == 1:
+            if s == 2:
                 nc.vector.quantize_mx(
                     out=x_codes[:].bitcast(FP8X4),
                     scales=x_scales[:],
                     in_=x_grouped[:].rearrange("p d t -> p (d t)"),
                 )
             if 0 <= s - LAG < QUADS:
-                multiply(s - LAG)
-                if not e_on_vector(s - LAG):
-                    store(s - LAG, nc.scalar.copy)
+                for first, last in pieces(s - LAG):
+                    multiply(s - LAG, first, last)
+                    if last < GROUP or not e_on_vector(s - LAG):
+                        store(s - LAG, first, last, nc.scalar.copy)
             if s < QUADS:
                 grouped_t[s] = qpool.tile([P, GROUP, P, PACK], BF16, name="grouped", align_bytes=64)
                 for j in range(GROUP):
@@ -225,3 +236,5 @@ def tile_nntransformlearner_pb_t_kernel(tc, G, x_next, out):
                 for j in range(GROUP):
                     if not c_on_vector(s * GROUP + j):
                         regroup(s * GROUP + j, nc.scalar.copy)
+            if s == 0:
+                nc.scalar.copy(out=x_grouped[:], in_=x_raw[:].rearrange("p t d -> p d t"))

from contextlib import ExitStack

import concourse.mybir as mybir
from concourse.masks import make_identity

F32 = mybir.dt.float32
BF16 = mybir.dt.bfloat16
U32 = mybir.dt.uint32
U8 = mybir.dt.uint8
FP8X4 = mybir.dt.float8_e4m3fn_x4
MULT = mybir.AluOpType.mult
ADD = mybir.AluOpType.add

P = 128
M, K, D = 16384, 512, 128
PACK = 4
TILES = M // P
GROUP = 4
QUADS = TILES // GROUP
FLOPS = 2 * M * K * D

LAG = 4
AHEAD = 8
TAIL_C = 1
TAIL_E = 1
E_ON_V_EVERY = 0
S_SUM_TILE = 1
S_SUM_EVERY = 8
S_SUM_AHEAD = 2
COPY = mybir.ActivationFunctionType.Copy


def tile_nntransformlearner_pb_t_kernel(tc, G, x_next, out):
    nc = tc.nc
    g_view = G.rearrange("(p c) k -> p c k", c=TILES)
    out_view = out.rearrange("(p c) d -> p c d", c=TILES)
    with ExitStack() as ctx:
        const = ctx.enter_context(tc.tile_pool(name="const", bufs=1))
        gpool = ctx.enter_context(tc.tile_pool(name="gpool", bufs=AHEAD + 2))
        small = ctx.enter_context(tc.tile_pool(name="small", bufs=6))
        ppool = ctx.enter_context(tc.tile_pool(name="ppool", bufs=3))
        qpool = ctx.enter_context(tc.tile_pool(name="qpool", bufs=LAG + 2))
        cpool = ctx.enter_context(tc.tile_pool(name="cpool", bufs=3))
        opool = ctx.enter_context(tc.tile_pool(name="opool", bufs=4))
        psum_t = ctx.enter_context(tc.psum_pool(name="psum_t", bufs=5))
        psum_o = ctx.enter_context(tc.psum_pool(name="psum_o", bufs=3))
        ctx.enter_context(tc.manual_schedule())

        g_tiles = {}
        sums_t = {}
        recip_t = {}
        p_tiles = {}
        xt_t = {}
        grouped_t = {}
        codes_t = {}
        scales_t = {}
        acc_t = {}

        def e_on_vector(q):
            if q >= QUADS - TAIL_E:
                return True
            return E_ON_V_EVERY > 0 and q % E_ON_V_EVERY == E_ON_V_EVERY - 1

        def c_on_vector(n):
            return n >= TILES - GROUP * TAIL_C and n % 2 == 1

        def sum_on_scalar(n):
            q, j = divmod(n, GROUP)
            if j != S_SUM_TILE or q == 0 or q >= QUADS:
                return False
            return q <= 2 or q % S_SUM_EVERY == S_SUM_EVERY - 1

        def pieces(q):
            if q == QUADS - 1:
                return [(0, GROUP // 2), (GROUP // 2, GROUP)]
            return [(0, GROUP)]

        def load(q):
            g_sb = gpool.tile([P, GROUP, K], BF16, name="g_sb")
            g_tiles[q] = g_sb
            if q == 0:
                for j in range(GROUP):
                    nc.sync.dma_start(out=g_sb[:, j, :], in_=g_view[:, j, :])
            else:
                nc.sync.dma_start(out=g_sb[:], in_=g_view[:, q * GROUP : (q + 1) * GROUP, :])

        def new_quad(q):
            sums_t[q] = small.tile([P, GROUP, 8], F32, name="sums")
            recip_t[q] = small.tile([P, GROUP], F32, name="recip")

        def row_sum_scalar(n):
            q, j = divmod(n, GROUP)
            nc.scalar.activation(
                out=junk_s[:, q % 2, :],
                in_=g_tiles[q][:, j, :],
                func=COPY,
                accum_out=sums_t[q][:, j, 0:1],
            )

        def row_sum(n):
            q, j = divmod(n, GROUP)
            if j == 0:
                p_tiles[q] = ppool.tile([P, GROUP, K], BF16, name="p_sb")
            if sum_on_scalar(n):
                return
            nc.vector.scalar_tensor_tensor(
                out=junk[:, j, :],
                in0=g_tiles[q][:, j, 0 : K // 2],
                scalar=1.0,
                in1=g_tiles[q][:, j, K // 2 : K],
                op0=MULT,
                op1=ADD,
                accum_out=sums_t[q][:, j, 0:1],
            )

        def reciprocals(q, first, last):
            nc.vector.reciprocal(recip_t[q][:, first:last], sums_t[q][:, first:last, 0])

        def normalise(n):
            q, j = divmod(n, GROUP)
            nc.vector.tensor_scalar(
                out=p_tiles[q][:, j, :],
                in0=g_tiles[q][:, j, :],
                scalar1=recip_t[q][:, j : j + 1],
                scalar2=None,
                op0=MULT,
            )

        def transpose(n):
            q, j = divmod(n, GROUP)
            xt = psum_t.tile([P, PACK, P], BF16, name="xt")
            xt_t[n] = xt
            for t in range(PACK):
                nc.tensor.transpose(xt[:, t, :], p_tiles[q][:, j, t * P : (t + 1) * P], ident[:])

        def regroup(n, engine_copy):
            q, j = divmod(n, GROUP)
            engine_copy(out=grouped_t[q][:, j, :, :], in_=xt_t[n][:].rearrange("p t m -> p m t"))

        def quantise(q, first, last):
            if first == 0:
                codes_t[q] = cpool.tile([P, GROUP * P], U32, name="codes", align_bytes=64)
                scales_t[q] = cpool.tile([P, GROUP * P], U8, name="scales", align_bytes=64)
            nc.vector.quantize_mx(
                out=codes_t[q][:, first * P : last * P].bitcast(FP8X4),
                scales=scales_t[q][:, first * P : last * P],
                in_=grouped_t[q][:, first:last, :, :].rearrange("p j m t -> p (j m t)"),
            )

        def multiply(q, first, last):
            acc_t[q, first] = psum_o.tile([P, GROUP, D], F32, name="acc")
            for j in range(first, last):
                nc.tensor.matmul_mx(
                    out=acc_t[q, first][:, j, :],
                    lhsT=codes_t[q][:, j * P : (j + 1) * P].bitcast(FP8X4),
                    lhsT_scale=scales_t[q][:, j * P : (j + 1) * P],
                    rhs=x_codes[:].bitcast(FP8X4),
                    rhs_scale=x_scales[:],
                    start=True,
                    stop=True,
                )

        def store(q, first, last, engine_copy):
            o_sb = opool.tile([P, GROUP, D], F32, name="o_sb")
            engine_copy(out=o_sb[:, first:last, :], in_=acc_t[q, first][:, first:last, :])
            nc.sync.dma_start(
                out=out_view[:, q * GROUP + first : q * GROUP + last, :], in_=o_sb[:, first:last, :]
            )

        x_raw = const.tile([P, PACK, D], BF16)
        for q in range(AHEAD):
            load(q)
            if q == 1:
                nc.sync.dma_start(out=x_raw[:], in_=x_next.rearrange("(t p) d -> p t d", p=P))
        ident = const.tile([P, P], BF16)
        make_identity(nc, ident[:])
        junk = const.tile([P, GROUP, K // 2], F32)
        junk_s = const.tile([P, 2, K], BF16)
        x_grouped = const.tile([P, D, PACK], BF16, align_bytes=64)
        x_codes = const.tile([P, D], U32, align_bytes=64)
        x_scales = const.tile([P, D], U8, align_bytes=64)

        for q in range(S_SUM_AHEAD):
            new_quad(q)
            for j in range(GROUP):
                if sum_on_scalar(q * GROUP + j):
                    row_sum_scalar(q * GROUP + j)
        row_sum(0)
        for s in range(QUADS + LAG + 2):
            if s + AHEAD < QUADS:
                load(s + AHEAD)
            if s + S_SUM_AHEAD < QUADS:
                new_quad(s + S_SUM_AHEAD)
                for j in range(GROUP):
                    if sum_on_scalar((s + S_SUM_AHEAD) * GROUP + j):
                        row_sum_scalar((s + S_SUM_AHEAD) * GROUP + j)
            if s == 0:
                for j in range(GROUP):
                    row_sum(j + 1)
                    reciprocals(0, j, j + 1)
                    normalise(j)
            elif s < QUADS:
                for j in range(1, GROUP):
                    row_sum(s * GROUP + j)
            if 0 <= s - LAG < QUADS:
                for first, last in pieces(s - LAG):
                    quantise(s - LAG, first, last)
            if 0 <= s - 1 < QUADS:
                for j in range(GROUP):
                    if c_on_vector((s - 1) * GROUP + j):
                        regroup((s - 1) * GROUP + j, nc.vector.tensor_copy)
            if 0 <= s - LAG - 1 < QUADS and e_on_vector(s - LAG - 1):
                first, last = pieces(s - LAG - 1)[-1]
                store(s - LAG - 1, first, last, nc.vector.tensor_copy)
            if 0 < s < QUADS:
                reciprocals(s, 0, GROUP)
                if s + 1 < QUADS:
                    row_sum((s + 1) * GROUP)
                for j in range(GROUP):
                    normalise(s * GROUP + j)
            if s == 2:
                nc.vector.quantize_mx(
                    out=x_codes[:].bitcast(FP8X4),
                    scales=x_scales[:],
                    in_=x_grouped[:].rearrange("p d t -> p (d t)"),
                )
            if 0 <= s - LAG < QUADS:
                for first, last in pieces(s - LAG):
                    multiply(s - LAG, first, last)
                    if last < GROUP or not e_on_vector(s - LAG):
                        store(s - LAG, first, last, nc.scalar.copy)
            if s < QUADS:
                grouped_t[s] = qpool.tile([P, GROUP, P, PACK], BF16, name="grouped", align_bytes=64)
                for j in range(GROUP):
                    transpose(s * GROUP + j)
                for j in range(GROUP):
                    if not c_on_vector(s * GROUP + j):
                        regroup(s * GROUP + j, nc.scalar.copy)
            if s == 0:
                nc.scalar.copy(out=x_grouped[:], in_=x_raw[:].rearrange("p t d -> p d t"))
